import numpy as np
import ml_dtypes


def mxq(x, axis, fmt="e4m3"):
    dtype, down = {"e4m3": (ml_dtypes.float8_e4m3fn, 7), "e5m2": (ml_dtypes.float8_e5m2, 14)}[fmt]
    v = np.moveaxis(np.asarray(x, np.float32).astype(ml_dtypes.bfloat16).astype(np.float64), axis, -1)
    blocks = v.reshape(v.shape[:-1] + (-1, 32))
    amax = np.abs(blocks).max(-1, keepdims=True)
    byte = np.maximum(np.where(amax > 0, np.frexp(amax)[1] - 1 + 127, 0) - down, 1)
    scale = np.exp2(byte - 127.0)
    codes = (blocks / scale).astype(np.float32).astype(dtype).astype(np.float64)
    return np.moveaxis((codes * scale).reshape(v.shape), -1, axis)


WIDE = False


def mx_kscale(k):
    if not WIDE:
        return np.ones(k)
    levels = np.array([10, -10, 5, -5, 0])
    a = np.random.permutation(np.resize(levels, k // 512 * 4)).reshape(k // 512, 4)
    idx = np.arange(k)
    return np.exp2(a[idx // 512, idx % 128 // 32])


BF16 = ml_dtypes.bfloat16


def bf(x):
    return np.asarray(x, np.float32).astype(BF16)


def f64(x):
    return np.asarray(x).astype(np.float64)


B, C, V, K, OUT = 4, 128, 2048, 4, 128


def setup_inputs():
    s = mx_kscale(V)
    g = np.random.standard_normal((V, V))
    lap = (g + g.T) * (0.45 / np.sqrt(V))
    return {"input": bf(np.random.standard_normal((B, C, V)) * s),
            "laplacian": bf(lap * s[:, None] / s[None, :])}


def reference(input, laplacian):
    x0 = f64(input).transpose(2, 1, 0).reshape(V, C * B)
    lq = mxq(f64(laplacian), 1, "e4m3")
    x1 = lq @ mxq(x0, 0, "e4m3")
    x2 = 2.0 * (lq @ mxq(x1, 0, "e4m3")) - x0
    return x1, x2

@@ -1,0 +1,192 @@
+from contextlib import ExitStack
+
+import concourse.mybir as mybir
+from concourse.masks import make_identity
+
+F32 = mybir.dt.float32
+BF16 = mybir.dt.bfloat16
+U32 = mybir.dt.uint32
+U8 = mybir.dt.uint8
+FP8X4 = mybir.dt.float8_e4m3fn_x4
+
+P = 128
+PACK = 4
+V = 2048
+BATCH = 4
+COLS = 512
+PASSES = V // (P * PACK)
+ROW_TILES = V // P
+PAIRS = ROW_TILES // 2
+ROW_WORDS = V // 2
+TILE_CODES = PASSES * P
+PSUM_BANKS = 8
+
+FLOPS = 2 * 2 * V * V * COLS
+
+
+def tile_graph_conv_pa_kernel(tc, signal, laplacian, x1_out, x2_out):
+    nc = tc.nc
+    with ExitStack() as ctx:
+        keep = ctx.enter_context(tc.tile_pool(name="keep", bufs=1))
+        lap_rows = ctx.enter_context(tc.tile_pool(name="lap_rows", bufs=PAIRS))
+        lap_stage = ctx.enter_context(tc.tile_pool(name="lap_stage", bufs=2))
+        x1_stage = ctx.enter_context(tc.tile_pool(name="x1_stage", bufs=2))
+        x2_stage = ctx.enter_context(tc.tile_pool(name="x2_stage", bufs=3))
+        psum = ctx.enter_context(tc.psum_pool(name="psum", bufs=PSUM_BANKS))
+        ctx.enter_context(tc.manual_schedule())
+
+        identity = keep.tile([P, P], F32)
+        signal_rows = keep.tile([P, BATCH * V], BF16)
+        x0_grouped = keep.tile([P, PASSES * COLS * PACK], BF16, align_bytes=64)
+        x0_codes = keep.tile([P, PASSES * COLS], U32, align_bytes=64)
+        x0_scales = keep.tile([P, PASSES * COLS], U8, align_bytes=64)
+        x1_codes = keep.tile([P, PASSES * COLS], U32, align_bytes=64)
+        x1_scales = keep.tile([P, PASSES * COLS], U8, align_bytes=64)
+        lap_codes = keep.tile([P, ROW_TILES * TILE_CODES], U32, align_bytes=64)
+        lap_scales = keep.tile([P, ROW_TILES * TILE_CODES], U8, align_bytes=64)
+
+        for b in range(BATCH):
+            nc.sync.dma_start(out=signal_rows[:, b * V : (b + 1) * V], in_=signal[b, :, :])
+        lap_pairs = []
+        for r in range(PAIRS):
+            pair_rows = lap_rows.tile([P, 2 * V], BF16, name="pair_rows")
+            nc.sync.dma_start(
+                out=pair_rows[:],
+                in_=laplacian[2 * P * r : 2 * P * (r + 1), :].rearrange("(p e) k -> p (e k)", e=2),
+            )
+            lap_pairs.append(pair_rows)
+
+        make_identity(nc, identity[:])
+
+        def new_bank():
+            return psum.tile([P, COLS], F32, name="bank")
+
+        def transpose_words(bank, j, words, first_word):
+            nc.tensor.transpose(
+                bank[:, j * P : (j + 1) * P], words[:, first_word : first_word + P], identity[:]
+            )
+
+        signal_words = signal_rows[:].bitcast(F32)
+        x0_words = x0_grouped[:].bitcast(F32).rearrange(
+            "p (g c b u) -> p g c b u", g=PASSES, c=P, b=BATCH, u=2
+        )
+        for h in range(2):
+            banks = []
+            for g in range(PASSES):
+                banks.append(new_bank())
+            for b in (2 * h, 2 * h + 1):
+                for g in range(PASSES):
+                    for u in range(2):
+                        transpose_words(
+                            banks[g], 2 * (b % 2) + u, signal_words, b * ROW_WORDS + (2 * g + u) * P
+                        )
+            for g in range(PASSES):
+                copy = nc.scalar.copy if g % 2 == 0 else nc.vector.tensor_copy
+                copy(
+                    out=x0_words[:, g, :, 2 * h : 2 * h + 2, :],
+                    in_=banks[g][:].rearrange("p (b u c) -> p c b u", b=2, u=2),
+                )
+        for g in range(PASSES):
+            nc.vector.quantize_mx(
+                out=x0_codes[:, g * COLS : (g + 1) * COLS].bitcast(FP8X4),
+                scales=x0_scales[:, g * COLS : (g + 1) * COLS],
+                in_=x0_grouped[:, g * COLS * PACK : (g + 1) * COLS * PACK],
+            )
+
+        def quantise_pair(r):
+            words = lap_pairs[r][:].bitcast(F32)
+            grouped = lap_stage.tile([P, 2 * TILE_CODES * PACK], BF16, name="grouped", align_bytes=64)
+            grouped_words = grouped[:].bitcast(F32).rearrange(
+                "p (n g i u) -> p n g i u", n=4, g=2, i=P, u=2
+            )
+            banks = []
+            for n in range(4):
+                bank = new_bank()
+                for j in range(4):
+                    transpose_words(bank, j, words, (4 * n + j) * P)
+                banks.append(bank)
+            for n in range(4):
+                nc.scalar.copy(
+                    out=grouped_words[:, n],
+                    in_=banks[n][:].rearrange("p (g u i) -> p g i u", g=2, u=2),
+                )
+            for e in range(2):
+                m = 2 * r + e
+                nc.vector.quantize_mx(
+                    out=lap_codes[:, m * TILE_CODES : (m + 1) * TILE_CODES].bitcast(FP8X4),
+                    scales=lap_scales[:, m * TILE_CODES : (m + 1) * TILE_CODES],
+                    in_=grouped[:, e * TILE_CODES * PACK : (e + 1) * TILE_CODES * PACK],
+                )
+
+        def multiply(acc, m, g, x_codes, x_scales):
+            rows = slice((m * PASSES + g) * P, (m * PASSES + g + 1) * P)
+            cols = slice(g * COLS, (g + 1) * COLS)
+            nc.tensor.matmul_mx(
+                out=acc[:],
+                lhsT=lap_codes[:, rows].bitcast(FP8X4),
+                lhsT_scale=lap_scales[:, rows],
+                rhs=x_codes[:, cols].bitcast(FP8X4),
+                rhs_scale=x_scales[:, cols],
+                start=(g == 0),
+                stop=(g == PASSES - 1),
+            )
+
+        def pair_of_rows(out, r):
+            return out[2 * P * r : 2 * P * (r + 1), :].rearrange("(p e) c -> p e c", e=2)
+
+        quantise_pair(0)
+        x1_rows = None
+        for r in range(PAIRS):
+            if r + 1 < PAIRS:
+                quantise_pair(r + 1)
+            g_out, u_out = divmod(r, 2)
+            if u_out == 0:
+                x1_rows = x1_stage.tile([P, PACK, COLS], F32, name="x1_rows")
+            for e in range(2):
+                acc = new_bank()
+                for g in range(PASSES):
+                    multiply(acc, 2 * r + e, g, x0_codes, x0_scales)
+                nc.scalar.copy(out=x1_rows[:, 2 * u_out + e, :], in_=acc[:])
+            nc.sync.dma_start(out=pair_of_rows(x1_out, r), in_=x1_rows[:, 2 * u_out : 2 * u_out + 2, :])
+            if u_out == 1:
+                x1_grouped = x1_stage.tile([P, COLS, PACK], BF16, name="x1_grouped", align_bytes=64)
+                nc.vector.tensor_copy(out=x1_grouped[:], in_=x1_rows[:].rearrange("p t c -> p c t"))
+                nc.vector.quantize_mx(
+                    out=x1_codes[:, g_out * COLS : (g_out + 1) * COLS].bitcast(FP8X4),
+                    scales=x1_scales[:, g_out * COLS : (g_out + 1) * COLS],
+                    in_=x1_grouped[:].rearrange("p c t -> p (c t)"),
+                )
+
+        x0_values = x0_grouped[:].rearrange("p (g c t) -> p g c t", g=PASSES, c=COLS, t=PACK)
+        x2_rows_of_pair = {}
+
+        def finish_x2(acc, m):
+            r, e = divmod(m, 2)
+            g_out, u_out = divmod(r, 2)
+            if e == 0:
+                x2_rows_of_pair[r] = x2_stage.tile([P, 2, COLS], F32, name="x2_rows")
+            x2_rows = x2_rows_of_pair[r]
+            nc.vector.scalar_tensor_tensor(
+                out=x2_rows[:, e, :],
+                in0=acc[:],
+                scalar=2.0,
+                in1=x0_values[:, g_out, :, 2 * u_out + e],
+                op0=mybir.AluOpType.mult,
+                op1=mybir.AluOpType.subtract,
+            )
+            if e == 1:
+                nc.sync.dma_start(out=pair_of_rows(x2_out, r), in_=x2_rows[:])
+
+        accs = []
+        for m in range(PSUM_BANKS):
+            accs.append(new_bank())
+        for g in range(PASSES):
+            for m in range(PSUM_BANKS):
+                multiply(accs[m], m, g, x1_codes, x1_scales)
+                if g == PASSES - 1:
+                    finish_x2(accs[m], m)
+        for m in range(PSUM_BANKS, ROW_TILES):
+            acc = new_bank()
+            for g in range(PASSES):
+                multiply(acc, m, g, x1_codes, x1_scales)
+            finish_x2(acc, m)

@@ -31,12 +31,12 @@ def tile_graph_conv_pa_kernel(tc, signal, laplacian, x1_out, x2_out):
         lap_rows = ctx.enter_context(tc.tile_pool(name="lap_rows", bufs=PAIRS))
         lap_stage = ctx.enter_context(tc.tile_pool(name="lap_stage", bufs=2))
         x1_stage = ctx.enter_context(tc.tile_pool(name="x1_stage", bufs=2))
-        x2_stage = ctx.enter_context(tc.tile_pool(name="x2_stage", bufs=3))
+        x2_stage = ctx.enter_context(tc.tile_pool(name="x2_stage", bufs=4))
         psum = ctx.enter_context(tc.psum_pool(name="psum", bufs=PSUM_BANKS))
         ctx.enter_context(tc.manual_schedule())
 
         identity = keep.tile([P, P], F32)
-        signal_rows = keep.tile([P, BATCH * V], BF16)
+        signal_rows = keep.tile([P, PASSES, BATCH, P * PACK], BF16)
         x0_grouped = keep.tile([P, PASSES * COLS * PACK], BF16, align_bytes=64)
         x0_codes = keep.tile([P, PASSES * COLS], U32, align_bytes=64)
         x0_scales = keep.tile([P, PASSES * COLS], U8, align_bytes=64)
@@ -45,8 +45,6 @@ def tile_graph_conv_pa_kernel(tc, signal, laplacian, x1_out, x2_out):
         lap_codes = keep.tile([P, ROW_TILES * TILE_CODES], U32, align_bytes=64)
         lap_scales = keep.tile([P, ROW_TILES * TILE_CODES], U8, align_bytes=64)
 
-        for b in range(BATCH):
-            nc.sync.dma_start(out=signal_rows[:, b * V : (b + 1) * V], in_=signal[b, :, :])
         lap_pairs = []
         for r in range(PAIRS):
             pair_rows = lap_rows.tile([P, 2 * V], BF16, name="pair_rows")
@@ -55,6 +53,12 @@ def tile_graph_conv_pa_kernel(tc, signal, laplacian, x1_out, x2_out):
                 in_=laplacian[2 * P * r : 2 * P * (r + 1), :].rearrange("(p e) k -> p (e k)", e=2),
             )
             lap_pairs.append(pair_rows)
+            if r == 0:
+                for g in range(PASSES):
+                    nc.sync.dma_start(
+                        out=signal_rows[:, g, :, :],
+                        in_=signal[:, :, g * P * PACK : (g + 1) * P * PACK].rearrange("b c v -> c b v"),
+                    )
 
         make_identity(nc, identity[:])
 
@@ -66,27 +70,21 @@ def tile_graph_conv_pa_kernel(tc, signal, laplacian, x1_out, x2_out):
                 bank[:, j * P : (j + 1) * P], words[:, first_word : first_word + P], identity[:]
             )
 
-        signal_words = signal_rows[:].bitcast(F32)
+        signal_words = signal_rows[:].rearrange("p g b v -> p (g b v)").bitcast(F32)
         x0_words = x0_grouped[:].bitcast(F32).rearrange(
             "p (g c b u) -> p g c b u", g=PASSES, c=P, b=BATCH, u=2
         )
-        for h in range(2):
-            banks = []
-            for g in range(PASSES):
-                banks.append(new_bank())
-            for b in (2 * h, 2 * h + 1):
-                for g in range(PASSES):
-                    for u in range(2):
-                        transpose_words(
-                            banks[g], 2 * (b % 2) + u, signal_words, b * ROW_WORDS + (2 * g + u) * P
-                        )
-            for g in range(PASSES):
-                copy = nc.scalar.copy if g % 2 == 0 else nc.vector.tensor_copy
+
+        def quantise_x0(g):
+            copy = nc.scalar.copy if g % 2 == 0 else nc.vector.tensor_copy
+            for h in range(2):
+                bank = new_bank()
+                for j in range(4):
+                    transpose_words(bank, j, signal_words, ((g * 2 + h) * 4 + j) * P)
                 copy(
                     out=x0_words[:, g, :, 2 * h : 2 * h + 2, :],
-                    in_=banks[g][:].rearrange("p (b u c) -> p c b u", b=2, u=2),
+                    in_=bank[:].rearrange("p (b u c) -> p c b u", b=2, u=2),
                 )
-        for g in range(PASSES):
             nc.vector.quantize_mx(
                 out=x0_codes[:, g * COLS : (g + 1) * COLS].bitcast(FP8X4),
                 scales=x0_scales[:, g * COLS : (g + 1) * COLS],
@@ -106,7 +104,8 @@ def tile_graph_conv_pa_kernel(tc, signal, laplacian, x1_out, x2_out):
                     transpose_words(bank, j, words, (4 * n + j) * P)
                 banks.append(bank)
             for n in range(4):
-                nc.scalar.copy(
+                copy = nc.scalar.copy if n < 3 else nc.vector.tensor_copy
+                copy(
                     out=grouped_words[:, n],
                     in_=banks[n][:].rearrange("p (g u i) -> p g i u", g=2, u=2),
                 )
@@ -131,24 +130,30 @@ def tile_graph_conv_pa_kernel(tc, signal, laplacian, x1_out, x2_out):
                 stop=(g == PASSES - 1),
             )
 
-        def pair_of_rows(out, r):
+        def multiply_tiles(tiles, x_codes, x_scales, finish):
+            accs = {}
+            for m in tiles:
+                accs[m] = new_bank()
+            for g in range(PASSES):
+                for m in tiles:
+                    multiply(accs[m], m, g, x_codes, x_scales)
+                    if g == PASSES - 1:
+                        finish(accs[m], m)
+
+        def rows_of_pair(out, r):
             return out[2 * P * r : 2 * P * (r + 1), :].rearrange("(p e) c -> p e c", e=2)
 
-        quantise_pair(0)
-        x1_rows = None
-        for r in range(PAIRS):
-            if r + 1 < PAIRS:
-                quantise_pair(r + 1)
-            g_out, u_out = divmod(r, 2)
-            if u_out == 0:
-                x1_rows = x1_stage.tile([P, PACK, COLS], F32, name="x1_rows")
-            for e in range(2):
-                acc = new_bank()
-                for g in range(PASSES):
-                    multiply(acc, 2 * r + e, g, x0_codes, x0_scales)
-                nc.scalar.copy(out=x1_rows[:, 2 * u_out + e, :], in_=acc[:])
-            nc.sync.dma_start(out=pair_of_rows(x1_out, r), in_=x1_rows[:, 2 * u_out : 2 * u_out + 2, :])
-            if u_out == 1:
+        x1_rows_of_pass = {}
+
+        def finish_x1(acc, m):
+            g_out, t = divmod(m, PACK)
+            if t == 0:
+                x1_rows_of_pass[g_out] = x1_stage.tile([P, PACK, COLS], F32, name="x1_rows")
+            x1_rows = x1_rows_of_pass[g_out]
+            nc.scalar.copy(out=x1_rows[:, t, :], in_=acc[:])
+            if t % 2 == 1:
+                nc.sync.dma_start(out=rows_of_pair(x1_out, m // 2), in_=x1_rows[:, t - 1 : t + 1, :])
+            if t == PACK - 1:
                 x1_grouped = x1_stage.tile([P, COLS, PACK], BF16, name="x1_grouped", align_bytes=64)
                 nc.vector.tensor_copy(out=x1_grouped[:], in_=x1_rows[:].rearrange("p t c -> p c t"))
                 nc.vector.quantize_mx(
@@ -157,36 +162,32 @@ def tile_graph_conv_pa_kernel(tc, signal, laplacian, x1_out, x2_out):
                     in_=x1_grouped[:].rearrange("p c t -> p (c t)"),
                 )
 
+        quantise_pair(0)
+        for g in range(PASSES):
+            quantise_x0(g)
+        multiply_tiles((0, 1), x0_codes, x0_scales, finish_x1)
+        quantise_pair(1)
+        for r in range(1, PAIRS):
+            if r + 1 < PAIRS:
+                quantise_pair(r + 1)
+            for e in range(2):
+                multiply_tiles((2 * r + e,), x0_codes, x0_scales, finish_x1)
+
         x0_values = x0_grouped[:].rearrange("p (g c t) -> p g c t", g=PASSES, c=COLS, t=PACK)
-        x2_rows_of_pair = {}
 
         def finish_x2(acc, m):
-            r, e = divmod(m, 2)
-            g_out, u_out = divmod(r, 2)
-            if e == 0:
-                x2_rows_of_pair[r] = x2_stage.tile([P, 2, COLS], F32, name="x2_rows")
-            x2_rows = x2_rows_of_pair[r]
+            g_out, t = divmod(m, PACK)
+            x2_rows = x2_stage.tile([P, COLS], F32, name="x2_rows")
             nc.vector.scalar_tensor_tensor(
-                out=x2_rows[:, e, :],
+                out=x2_rows[:],
                 in0=acc[:],
                 scalar=2.0,
-                in1=x0_values[:, g_out, :, 2 * u_out + e],
+                in1=x0_values[:, g_out, :, t],
                 op0=mybir.AluOpType.mult,
                 op1=mybir.AluOpType.subtract,
             )
-            if e == 1:
-                nc.sync.dma_start(out=pair_of_rows(x2_out, r), in_=x2_rows[:])
+            nc.sync.dma_start(out=rows_of_pair(x2_out, m // 2)[:, m % 2, :], in_=x2_rows[:])
 
-        accs = []
-        for m in range(PSUM_BANKS):
-            accs.append(new_bank())
-        for g in range(PASSES):
-            for m in range(PSUM_BANKS):
-                multiply(accs[m], m, g, x1_codes, x1_scales)
-                if g == PASSES - 1:
-                    finish_x2(accs[m], m)
+        multiply_tiles(range(PSUM_BANKS), x1_codes, x1_scales, finish_x2)
         for m in range(PSUM_BANKS, ROW_TILES):
-            acc = new_bank()
-            for g in range(PASSES):
-                multiply(acc, m, g, x1_codes, x1_scales)
-            finish_x2(acc, m)
+            multiply_tiles((m,), x1_codes, x1_scales, finish_x2)

@@ -20,6 +20,7 @@ PAIRS = ROW_TILES // 2
 ROW_WORDS = V // 2
 TILE_CODES = PASSES * P
 PSUM_BANKS = 8
+WARM_UP = 12
 
 FLOPS = 2 * 2 * V * V * COLS
 
@@ -69,6 +70,14 @@ def tile_graph_conv_pa_kernel(tc, signal, laplacian, x1_out, x2_out):
             nc.tensor.transpose(
                 bank[:, j * P : (j + 1) * P], words[:, first_word : first_word + P], identity[:]
             )
+
+        zeros = keep.tile([P, COLS], BF16)
+        nc.vector.memset(zeros[:], 0.0)
+        unread_bank = new_bank()
+
+        def idle_matmuls(count):
+            for i in range(count):
+                nc.tensor.matmul(unread_bank[:], lhsT=zeros[:, 0:P], rhs=zeros[:], start=True, stop=True)
 
         signal_words = signal_rows[:].rearrange("p g b v -> p (g b v)").bitcast(F32)
         x0_words = x0_grouped[:].bitcast(F32).rearrange(
@@ -162,9 +171,12 @@ def tile_graph_conv_pa_kernel(tc, signal, laplacian, x1_out, x2_out):
                     in_=x1_grouped[:].rearrange("p c t -> p (c t)"),
                 )
 
+        idle_matmuls(WARM_UP)
         quantise_pair(0)
+        idle_matmuls(2)
         for g in range(PASSES):
             quantise_x0(g)
+            idle_matmuls(1)
         multiply_tiles((0, 1), x0_codes, x0_scales, finish_x1)
         quantise_pair(1)
         for r in range(1, PAIRS):

from contextlib import ExitStack

import concourse.mybir as mybir
from concourse.masks import make_identity

F32 = mybir.dt.float32
BF16 = mybir.dt.bfloat16
U32 = mybir.dt.uint32
U8 = mybir.dt.uint8
FP8X4 = mybir.dt.float8_e4m3fn_x4

P = 128
PACK = 4
V = 2048
BATCH = 4
COLS = 512
PASSES = V // (P * PACK)
ROW_TILES = V // P
PAIRS = ROW_TILES // 2
ROW_WORDS = V // 2
TILE_CODES = PASSES * P
PSUM_BANKS = 8
WARM_UP = 12

FLOPS = 2 * 2 * V * V * COLS


def tile_graph_conv_pa_kernel(tc, signal, laplacian, x1_out, x2_out):
    nc = tc.nc
    with ExitStack() as ctx:
        keep = ctx.enter_context(tc.tile_pool(name="keep", bufs=1))
        lap_rows = ctx.enter_context(tc.tile_pool(name="lap_rows", bufs=PAIRS))
        lap_stage = ctx.enter_context(tc.tile_pool(name="lap_stage", bufs=2))
        x1_stage = ctx.enter_context(tc.tile_pool(name="x1_stage", bufs=2))
        x2_stage = ctx.enter_context(tc.tile_pool(name="x2_stage", bufs=4))
        psum = ctx.enter_context(tc.psum_pool(name="psum", bufs=PSUM_BANKS))
        ctx.enter_context(tc.manual_schedule())

        identity = keep.tile([P, P], F32)
        signal_rows = keep.tile([P, PASSES, BATCH, P * PACK], BF16)
        x0_grouped = keep.tile([P, PASSES * COLS * PACK], BF16, align_bytes=64)
        x0_codes = keep.tile([P, PASSES * COLS], U32, align_bytes=64)
        x0_scales = keep.tile([P, PASSES * COLS], U8, align_bytes=64)
        x1_codes = keep.tile([P, PASSES * COLS], U32, align_bytes=64)
        x1_scales = keep.tile([P, PASSES * COLS], U8, align_bytes=64)
        lap_codes = keep.tile([P, ROW_TILES * TILE_CODES], U32, align_bytes=64)
        lap_scales = keep.tile([P, ROW_TILES * TILE_CODES], U8, align_bytes=64)

        lap_pairs = []
        for r in range(PAIRS):
            pair_rows = lap_rows.tile([P, 2 * V], BF16, name="pair_rows")
            nc.sync.dma_start(
                out=pair_rows[:],
                in_=laplacian[2 * P * r : 2 * P * (r + 1), :].rearrange("(p e) k -> p (e k)", e=2),
            )
            lap_pairs.append(pair_rows)
            if r == 0:
                for g in range(PASSES):
                    nc.sync.dma_start(
                        out=signal_rows[:, g, :, :],
                        in_=signal[:, :, g * P * PACK : (g + 1) * P * PACK].rearrange("b c v -> c b v"),
                    )

        make_identity(nc, identity[:])

        def new_bank():
            return psum.tile([P, COLS], F32, name="bank")

        def transpose_words(bank, j, words, first_word):
            nc.tensor.transpose(
                bank[:, j * P : (j + 1) * P], words[:, first_word : first_word + P], identity[:]
            )

        zeros = keep.tile([P, COLS], BF16)
        nc.vector.memset(zeros[:], 0.0)
        unread_bank = new_bank()

        def idle_matmuls(count):
            for i in range(count):
                nc.tensor.matmul(unread_bank[:], lhsT=zeros[:, 0:P], rhs=zeros[:], start=True, stop=True)

        signal_words = signal_rows[:].rearrange("p g b v -> p (g b v)").bitcast(F32)
        x0_words = x0_grouped[:].bitcast(F32).rearrange(
            "p (g c b u) -> p g c b u", g=PASSES, c=P, b=BATCH, u=2
        )

        def quantise_x0(g):
            copy = nc.scalar.copy if g % 2 == 0 else nc.vector.tensor_copy
            for h in range(2):
                bank = new_bank()
                for j in range(4):
                    transpose_words(bank, j, signal_words, ((g * 2 + h) * 4 + j) * P)
                copy(
                    out=x0_words[:, g, :, 2 * h : 2 * h + 2, :],
                    in_=bank[:].rearrange("p (b u c) -> p c b u", b=2, u=2),
                )
            nc.vector.quantize_mx(
                out=x0_codes[:, g * COLS : (g + 1) * COLS].bitcast(FP8X4),
                scales=x0_scales[:, g * COLS : (g + 1) * COLS],
                in_=x0_grouped[:, g * COLS * PACK : (g + 1) * COLS * PACK],
            )

        def quantise_pair(r):
            words = lap_pairs[r][:].bitcast(F32)
            grouped = lap_stage.tile([P, 2 * TILE_CODES * PACK], BF16, name="grouped", align_bytes=64)
            grouped_words = grouped[:].bitcast(F32).rearrange(
                "p (n g i u) -> p n g i u", n=4, g=2, i=P, u=2
            )
            banks = []
            for n in range(4):
                bank = new_bank()
                for j in range(4):
                    transpose_words(bank, j, words, (4 * n + j) * P)
                banks.append(bank)
            for n in range(4):
                copy = nc.scalar.copy if n < 3 else nc.vector.tensor_copy
                copy(
                    out=grouped_words[:, n],
                    in_=banks[n][:].rearrange("p (g u i) -> p g i u", g=2, u=2),
                )
            for e in range(2):
                m = 2 * r + e
                nc.vector.quantize_mx(
                    out=lap_codes[:, m * TILE_CODES : (m + 1) * TILE_CODES].bitcast(FP8X4),
                    scales=lap_scales[:, m * TILE_CODES : (m + 1) * TILE_CODES],
                    in_=grouped[:, e * TILE_CODES * PACK : (e + 1) * TILE_CODES * PACK],
                )

        def multiply(acc, m, g, x_codes, x_scales):
            rows = slice((m * PASSES + g) * P, (m * PASSES + g + 1) * P)
            cols = slice(g * COLS, (g + 1) * COLS)
            nc.tensor.matmul_mx(
                out=acc[:],
                lhsT=lap_codes[:, rows].bitcast(FP8X4),
                lhsT_scale=lap_scales[:, rows],
                rhs=x_codes[:, cols].bitcast(FP8X4),
                rhs_scale=x_scales[:, cols],
                start=(g == 0),
                stop=(g == PASSES - 1),
            )

        def multiply_tiles(tiles, x_codes, x_scales, finish):
            accs = {}
            for m in tiles:
                accs[m] = new_bank()
            for g in range(PASSES):
                for m in tiles:
                    multiply(accs[m], m, g, x_codes, x_scales)
                    if g == PASSES - 1:
                        finish(accs[m], m)

        def rows_of_pair(out, r):
            return out[2 * P * r : 2 * P * (r + 1), :].rearrange("(p e) c -> p e c", e=2)

        x1_rows_of_pass = {}

        def finish_x1(acc, m):
            g_out, t = divmod(m, PACK)
            if t == 0:
                x1_rows_of_pass[g_out] = x1_stage.tile([P, PACK, COLS], F32, name="x1_rows")
            x1_rows = x1_rows_of_pass[g_out]
            nc.scalar.copy(out=x1_rows[:, t, :], in_=acc[:])
            if t % 2 == 1:
                nc.sync.dma_start(out=rows_of_pair(x1_out, m // 2), in_=x1_rows[:, t - 1 : t + 1, :])
            if t == PACK - 1:
                x1_grouped = x1_stage.tile([P, COLS, PACK], BF16, name="x1_grouped", align_bytes=64)
                nc.vector.tensor_copy(out=x1_grouped[:], in_=x1_rows[:].rearrange("p t c -> p c t"))
                nc.vector.quantize_mx(
                    out=x1_codes[:, g_out * COLS : (g_out + 1) * COLS].bitcast(FP8X4),
                    scales=x1_scales[:, g_out * COLS : (g_out + 1) * COLS],
                    in_=x1_grouped[:].rearrange("p c t -> p (c t)"),
                )

        idle_matmuls(WARM_UP)
        quantise_pair(0)
        idle_matmuls(2)
        for g in range(PASSES):
            quantise_x0(g)
            idle_matmuls(1)
        multiply_tiles((0, 1), x0_codes, x0_scales, finish_x1)
        quantise_pair(1)
        for r in range(1, PAIRS):
            if r + 1 < PAIRS:
                quantise_pair(r + 1)
            for e in range(2):
                multiply_tiles((2 * r + e,), x0_codes, x0_scales, finish_x1)

        x0_values = x0_grouped[:].rearrange("p (g c t) -> p g c t", g=PASSES, c=COLS, t=PACK)

        def finish_x2(acc, m):
            g_out, t = divmod(m, PACK)
            x2_rows = x2_stage.tile([P, COLS], F32, name="x2_rows")
            nc.vector.scalar_tensor_tensor(
                out=x2_rows[:],
                in0=acc[:],
                scalar=2.0,
                in1=x0_values[:, g_out, :, t],
                op0=mybir.AluOpType.mult,
                op1=mybir.AluOpType.subtract,
            )
            nc.sync.dma_start(out=rows_of_pair(x2_out, m // 2)[:, m % 2, :], in_=x2_rows[:])

        multiply_tiles(range(PSUM_BANKS), x1_codes, x1_scales, finish_x2)
        for m in range(PSUM_BANKS, ROW_TILES):
            multiply_tiles((m,), x1_codes, x1_scales, finish_x2)
